import numpy as np
import ml_dtypes


def mxq(x, axis, fmt="e4m3"):
    dtype, down = {"e4m3": (ml_dtypes.float8_e4m3fn, 7), "e5m2": (ml_dtypes.float8_e5m2, 14)}[fmt]
    v = np.moveaxis(np.asarray(x, np.float32).astype(ml_dtypes.bfloat16).astype(np.float64), axis, -1)
    blocks = v.reshape(v.shape[:-1] + (-1, 32))
    amax = np.abs(blocks).max(-1, keepdims=True)
    byte = np.maximum(np.where(amax > 0, np.frexp(amax)[1] - 1 + 127, 0) - down, 1)
    scale = np.exp2(byte - 127.0)
    codes = (blocks / scale).astype(np.float32).astype(dtype).astype(np.float64)
    return np.moveaxis((codes * scale).reshape(v.shape), -1, axis)


WIDE = False


def mx_kscale(k):
    if not WIDE:
        return np.ones(k)
    levels = np.array([10, -10, 5, -5, 0])
    a = np.random.permutation(np.resize(levels, k // 512 * 4)).reshape(k // 512, 4)
    idx = np.arange(k)
    return np.exp2(a[idx // 512, idx % 128 // 32])


BF16 = ml_dtypes.bfloat16


def bf(x):
    return np.asarray(x, np.float32).astype(BF16)


def f64(x):
    return np.asarray(x).astype(np.float64)


B, T, E, H, DK, C = 1, 1024, 1024, 4, 256, 512
DV = 2 * DK
F = H * DV
EPS = 1e-5


def setup_inputs():
    s, t = mx_kscale(E), mx_kscale(F)
    o = np.random.standard_normal((B, T, H, DV)) * 5.0 * np.exp(0.5 * np.random.standard_normal((B, T, H, 1)))
    return {"o_ret": bf(o),
            "x": bf(np.random.standard_normal((B, T, E)) * s),
            "Wg": bf(np.random.standard_normal((E, F)) / np.sqrt(E) / s[:, None] * t),
            "gn_weight": bf(1.0 + 0.1 * np.random.standard_normal(DV)),
            "Wo": bf(np.random.standard_normal((F, E)) / np.sqrt(F) / t[:, None])}


def reference(o_ret, x, Wg, gn_weight, Wo):
    o = f64(o_ret)
    rms = np.sqrt(np.mean(o * o, axis=-1, keepdims=True) + EPS)
    o = o / rms * f64(gn_weight)
    g = mxq(f64(x), 2, "e4m3") @ mxq(f64(Wg), 0, "e4m3")
    h = o.reshape(B, T, F) * g
    return mxq(h, 2, "e4m3") @ mxq(f64(Wo), 0, "e4m3")

@@ -1,0 +1,229 @@
+import concourse.mybir as mybir
+from concourse.masks import make_identity
+
+FP8X4 = mybir.dt.float8_e4m3fn_x4
+BF16 = mybir.dt.bfloat16
+F32 = mybir.dt.float32
+U32 = mybir.dt.uint32
+U8 = mybir.dt.uint8
+ACT = mybir.ActivationFunctionType
+ALU = mybir.AluOpType
+
+P = 128
+PACK = 4
+K_PASS = P * PACK
+T = 1024
+E = 1024
+HEADS = 4
+DV = 512
+F = HEADS * DV
+N_OUT = 1024
+N_TILE = 512
+T_TILES = T // P
+E_PASSES = E // K_PASS
+N_HALVES = N_OUT // N_TILE
+EPS = 1e-5
+
+FLOPS = 2 * T * E * F + 2 * T * F * N_OUT
+
+
+def regroup_and_quantise(nc, copy_engine_copy, stage, rows, codes, scales):
+    grouped = stage.tile([P, N_TILE, PACK], BF16, align_bytes=64, tag="w_grouped")
+    copy_engine_copy(
+        out=grouped[:].rearrange("p (c i) j -> p c j i", i=4),
+        in_=rows.rearrange("p j (c i) -> p c j i", i=4),
+    )
+    nc.vector.quantize_mx(
+        out=codes.bitcast(FP8X4),
+        scales=scales,
+        in_=grouped[:].rearrange("p w j -> p (w j)"),
+    )
+
+
+def tile_multiscaleretention_pc_kernel(tc, o_ret, x, Wg, gn_weight, Wo, out):
+    nc = tc.nc
+    x_view = x.flatten_outer_dims().rearrange("(p i) e -> p i e", i=T_TILES)
+    o_view = o_ret.rearrange("b t h d -> (b t) (h d)").rearrange("(p i) f -> p i f", i=T_TILES)
+    out_view = out.flatten_outer_dims().rearrange("(p i) n -> p i n", i=T_TILES)
+
+    with tc.tile_pool(name="keep", bufs=1) as keep, tc.tile_pool(name="stage", bufs=3) as stage, tc.tile_pool(
+        name="h0_pool", bufs=6
+    ) as h0_pool, tc.tile_pool(name="pair", bufs=2) as pair, tc.psum_pool(name="psum_g", bufs=3) as psum_g, tc.psum_pool(
+        name="psum_tr", bufs=3
+    ) as psum_tr, tc.psum_pool(name="psum_acc", bufs=2) as psum_acc:
+        ident = keep.tile([P, P], F32)
+        make_identity(nc, ident[:])
+        eps_col = keep.tile([P, 1], F32)
+        nc.vector.memset(eps_col[:], EPS)
+        gn_rows = keep.tile([P, P], BF16)
+        nc.vector.memset(gn_rows[:], 0.0)
+
+        x_raw = keep.tile([P, T_TILES, E], BF16)
+        wg_raw = keep.tile([P, E_PASSES, PACK, F], BF16)
+        o_raw = keep.tile([P, T_TILES, F], BF16)
+        wo_raw = keep.tile([P, HEADS, PACK, N_OUT], BF16)
+        nc.sync.dma_start(out=gn_rows[0:PACK, :], in_=gn_weight.rearrange("(j p) -> j p", p=P))
+        nc.sync.dma_start(out=x_raw[:, 0:4, :], in_=x_view[:, 0:4, :])
+        for c in range(E_PASSES):
+            for u in range(2):
+                first = K_PASS * c + 256 * u
+                nc.sync.dma_start(
+                    out=wg_raw[:, c, 2 * u : 2 * u + 2, :],
+                    in_=Wg[first : first + 256, :].rearrange("(q e) f -> q e f", e=2),
+                )
+        nc.sync.dma_start(out=o_raw[:, 0:2, :], in_=o_view[:, 0:2, :])
+        nc.sync.dma_start(out=x_raw[:, 4:8, :], in_=x_view[:, 4:8, :])
+        for a in range(1, 4):
+            nc.sync.dma_start(out=o_raw[:, 2 * a : 2 * a + 2, :], in_=o_view[:, 2 * a : 2 * a + 2, :])
+        for head in range(HEADS):
+            nc.sync.dma_start(
+                out=wo_raw[:, head, :, :],
+                in_=Wo[K_PASS * head : K_PASS * (head + 1), :].rearrange("(j p) n -> p j n", p=P),
+            )
+
+        gn_rows_f32 = keep.tile([P, P], F32)
+        nc.vector.tensor_copy(out=gn_rows_f32[:], in_=gn_rows[:])
+        gn_t = psum_tr.tile([P, PACK, P], F32, tag="tr")
+        nc.tensor.transpose(gn_t[:, 0, :], gn_rows_f32[:], ident[:])
+        gn_cols = keep.tile([P, PACK], F32)
+        nc.vector.tensor_copy(out=gn_cols[:], in_=gn_t[:, 0, 0:PACK])
+
+        x_words = x_raw[:].bitcast(F32)
+        x_codes = keep.tile([P, T_TILES, E_PASSES, P], U32, align_bytes=64)
+        x_scales = keep.tile([P, T_TILES, E_PASSES, P], U8, align_bytes=64)
+
+        def prepare_x(i):
+            xt = psum_tr.tile([P, PACK, P], F32, tag="tr")
+            for cu in range(PACK):
+                nc.tensor.transpose(xt[:, cu, :], x_words[:, i, P * cu : P * (cu + 1)], ident[:])
+            x_grouped = pair.tile([P, E_PASSES, P, PACK], BF16, align_bytes=64)
+            nc.scalar.copy(
+                out=x_grouped[:].bitcast(F32),
+                in_=xt[:].rearrange("p (c u) t -> p c t u", u=2),
+            )
+            nc.vector.quantize_mx(
+                out=x_codes[:, i, :, :].rearrange("p c t -> p (c t)").bitcast(FP8X4),
+                scales=x_scales[:, i, :, :].rearrange("p c t -> p (c t)"),
+                in_=x_grouped[:].rearrange("p c t j -> p (c t j)"),
+            )
+
+        wg_codes = keep.tile([P, E_PASSES, F], U32, align_bytes=64)
+        wg_scales = keep.tile([P, E_PASSES, F], U8, align_bytes=64)
+        wo_codes = keep.tile([P, HEADS, N_OUT], U32, align_bytes=64)
+        wo_scales = keep.tile([P, HEADS, N_OUT], U8, align_bytes=64)
+
+        for i in range(4):
+            prepare_x(i)
+        for c in range(E_PASSES):
+            for head in range(HEADS):
+                cols = slice(DV * head, DV * (head + 1))
+                copy = nc.vector.tensor_copy if head % 2 == 0 else nc.scalar.copy
+                regroup_and_quantise(
+                    nc, copy, stage, wg_raw[:, c, :, cols], wg_codes[:, c, cols], wg_scales[:, c, cols]
+                )
+        for i in range(4, T_TILES):
+            prepare_x(i)
+
+        rinv = []
+        for i in range(T_TILES):
+            ssq = keep.tile([P, HEADS], F32, name="ssq%d" % i)
+            for head in range(HEADS):
+                squares = stage.tile([P, DV], BF16, tag="squares")
+                nc.scalar.activation(
+                    out=squares[:],
+                    in_=o_raw[:, i, DV * head : DV * (head + 1)],
+                    func=ACT.Square,
+                    accum_out=ssq[:, head : head + 1],
+                )
+            rms = keep.tile([P, HEADS], F32, name="rms%d" % i)
+            nc.scalar.activation(out=rms[:], in_=ssq[:], func=ACT.Sqrt, scale=1.0 / DV, bias=eps_col[:])
+            rinv_i = keep.tile([P, HEADS], F32, name="rinv%d" % i)
+            nc.vector.reciprocal(out=rinv_i[:], in_=rms[:])
+            rinv.append(rinv_i)
+
+        for head in range(HEADS):
+            for half in range(N_HALVES):
+                cols = slice(N_TILE * half, N_TILE * (half + 1))
+                regroup_and_quantise(
+                    nc,
+                    nc.scalar.copy,
+                    stage,
+                    wo_raw[:, head, :, cols],
+                    wo_codes[:, head, cols],
+                    wo_scales[:, head, cols],
+                )
+
+        h_codes = keep.tile([P, T_TILES, HEADS, P], U32, align_bytes=64)
+        h_scales = keep.tile([P, T_TILES, HEADS, P], U8, align_bytes=64)
+        h0_tiles = {}
+
+        def gate_and_norm(i):
+            for head in range(HEADS):
+                cols = slice(DV * head, DV * (head + 1))
+                g = psum_g.tile([P, DV], F32)
+                for c in range(E_PASSES):
+                    nc.tensor.matmul_mx(
+                        out=g[:],
+                        lhsT=x_codes[:, i, c, :].bitcast(FP8X4),
+                        lhsT_scale=x_scales[:, i, c, :],
+                        rhs=wg_codes[:, c, cols].bitcast(FP8X4),
+                        rhs_scale=wg_scales[:, c, cols],
+                        start=(c == 0),
+                        stop=(c == E_PASSES - 1),
+                    )
+                h0 = h0_pool.tile([P, DV], F32)
+                nc.vector.scalar_tensor_tensor(
+                    out=h0[:],
+                    in0=g[:],
+                    scalar=rinv[i][:, head : head + 1],
+                    in1=o_raw[:, i, cols],
+                    op0=ALU.mult,
+                    op1=ALU.mult,
+                )
+                h0_tiles[(i, head)] = h0
+
+        def transpose_and_quantise(i):
+            h_grouped = pair.tile([P, HEADS, P, PACK], BF16, align_bytes=64)
+            for head in range(HEADS):
+                h0 = h0_tiles[(i, head)]
+                ht = psum_tr.tile([P, PACK, P], F32, tag="tr")
+                for j in range(PACK):
+                    nc.tensor.transpose(ht[:, j, :], h0[:, P * j : P * (j + 1)], ident[:])
+                nc.vector.tensor_tensor(
+                    out=h_grouped[:, head, :, :],
+                    in0=ht[:].rearrange("p j t -> p t j"),
+                    in1=gn_cols[:].unsqueeze(1).to_broadcast([P, P, PACK]),
+                    op=ALU.mult,
+                )
+            nc.vector.quantize_mx(
+                out=h_codes[:, i, :, :].rearrange("p h t -> p (h t)").bitcast(FP8X4),
+                scales=h_scales[:, i, :, :].rearrange("p h t -> p (h t)"),
+                in_=h_grouped[:].rearrange("p h t j -> p (h t j)"),
+            )
+
+        def project_and_store(i):
+            acc = [psum_acc.tile([P, N_TILE], F32, name="acc%d" % half, tag="acc") for half in range(N_HALVES)]
+            for head in range(HEADS):
+                for half in range(N_HALVES):
+                    cols = slice(N_TILE * half, N_TILE * (half + 1))
+                    nc.tensor.matmul_mx(
+                        out=acc[half][:],
+                        lhsT=h_codes[:, i, head, :].bitcast(FP8X4),
+                        lhsT_scale=h_scales[:, i, head, :],
+                        rhs=wo_codes[:, head, cols].bitcast(FP8X4),
+                        rhs_scale=wo_scales[:, head, cols],
+                        start=(head == 0),
+                        stop=(head == HEADS - 1),
+                    )
+            result = pair.tile([P, N_OUT], F32)
+            for half in range(N_HALVES):
+                nc.scalar.copy(out=result[:, N_TILE * half : N_TILE * (half + 1)], in_=acc[half][:])
+            nc.sync.dma_start(out=out_view[:, i, :], in_=result[:])
+
+        for step in range(T_TILES + 2):
+            if step < T_TILES:
+                gate_and_norm(step)
+            if 1 <= step <= T_TILES:
+                transpose_and_quantise(step - 1)
+            if step >= 2:
+                project_and_store(step - 2)

@@ -27,30 +27,19 @@ EPS = 1e-5
 FLOPS = 2 * T * E * F + 2 * T * F * N_OUT
 
 
-def regroup_and_quantise(nc, copy_engine_copy, stage, rows, codes, scales):
-    grouped = stage.tile([P, N_TILE, PACK], BF16, align_bytes=64, tag="w_grouped")
-    copy_engine_copy(
-        out=grouped[:].rearrange("p (c i) j -> p c j i", i=4),
-        in_=rows.rearrange("p j (c i) -> p c j i", i=4),
-    )
-    nc.vector.quantize_mx(
-        out=codes.bitcast(FP8X4),
-        scales=scales,
-        in_=grouped[:].rearrange("p w j -> p (w j)"),
-    )
-
-
 def tile_multiscaleretention_pc_kernel(tc, o_ret, x, Wg, gn_weight, Wo, out):
     nc = tc.nc
     x_view = x.flatten_outer_dims().rearrange("(p i) e -> p i e", i=T_TILES)
     o_view = o_ret.rearrange("b t h d -> (b t) (h d)").rearrange("(p i) f -> p i f", i=T_TILES)
     out_view = out.flatten_outer_dims().rearrange("(p i) n -> p i n", i=T_TILES)
 
-    with tc.tile_pool(name="keep", bufs=1) as keep, tc.tile_pool(name="stage", bufs=3) as stage, tc.tile_pool(
-        name="h0_pool", bufs=6
-    ) as h0_pool, tc.tile_pool(name="pair", bufs=2) as pair, tc.psum_pool(name="psum_g", bufs=3) as psum_g, tc.psum_pool(
-        name="psum_tr", bufs=3
-    ) as psum_tr, tc.psum_pool(name="psum_acc", bufs=2) as psum_acc:
+    with tc.tile_pool(name="keep", bufs=1) as keep, tc.tile_pool(name="w_stage", bufs=4) as w_stage, tc.tile_pool(
+        name="h0_pool", bufs=2 * HEADS
+    ) as h0_pool, tc.tile_pool(name="pair", bufs=2) as pair, tc.psum_pool(name="psum_g", bufs=2) as psum_g, tc.psum_pool(
+        name="psum_ht", bufs=3
+    ) as psum_ht, tc.psum_pool(name="psum_xt", bufs=1) as psum_xt, tc.psum_pool(
+        name="psum_acc", bufs=2
+    ) as psum_acc, tc.manual_schedule():
         ident = keep.tile([P, P], F32)
         make_identity(nc, ident[:])
         eps_col = keep.tile([P, 1], F32)
@@ -62,28 +51,49 @@ def tile_multiscaleretention_pc_kernel(tc, o_ret, x, Wg, gn_weight, Wo, out):
         wg_raw = keep.tile([P, E_PASSES, PACK, F], BF16)
         o_raw = keep.tile([P, T_TILES, F], BF16)
         wo_raw = keep.tile([P, HEADS, PACK, N_OUT], BF16)
-        nc.sync.dma_start(out=gn_rows[0:PACK, :], in_=gn_weight.rearrange("(j p) -> j p", p=P))
-        nc.sync.dma_start(out=x_raw[:, 0:4, :], in_=x_view[:, 0:4, :])
-        for c in range(E_PASSES):
-            for u in range(2):
-                first = K_PASS * c + 256 * u
-                nc.sync.dma_start(
-                    out=wg_raw[:, c, 2 * u : 2 * u + 2, :],
-                    in_=Wg[first : first + 256, :].rearrange("(q e) f -> q e f", e=2),
-                )
-        nc.sync.dma_start(out=o_raw[:, 0:2, :], in_=o_view[:, 0:2, :])
-        nc.sync.dma_start(out=x_raw[:, 4:8, :], in_=x_view[:, 4:8, :])
-        for a in range(1, 4):
-            nc.sync.dma_start(out=o_raw[:, 2 * a : 2 * a + 2, :], in_=o_view[:, 2 * a : 2 * a + 2, :])
-        for head in range(HEADS):
+
+        def load_x(i):
+            nc.sync.dma_start(out=x_raw[:, i, :], in_=x_view[:, i, :])
+
+        def load_o(i):
+            nc.sync.dma_start(out=o_raw[:, i, :], in_=o_view[:, i, :])
+
+        def load_wg(head_pair):
+            cols = slice(2 * DV * head_pair, 2 * DV * (head_pair + 1))
+            for c in range(E_PASSES):
+                for u in range(2):
+                    first = K_PASS * c + 256 * u
+                    nc.sync.dma_start(
+                        out=wg_raw[:, c, 2 * u : 2 * u + 2, cols],
+                        in_=Wg[first : first + 256, cols].rearrange("(q e) f -> q e f", e=2),
+                    )
+
+        def load_wo(head):
             nc.sync.dma_start(
                 out=wo_raw[:, head, :, :],
                 in_=Wo[K_PASS * head : K_PASS * (head + 1), :].rearrange("(j p) n -> p j n", p=P),
             )
 
+        nc.sync.dma_start(out=gn_rows[0:PACK, :], in_=gn_weight.rearrange("(j p) -> j p", p=P))
+        load_x(0)
+        load_o(0)
+        load_x(1)
+        load_wg(0)
+        load_wg(1)
+        load_o(1)
+        load_wo(0)
+        load_wo(1)
+        load_x(2)
+        load_o(2)
+        load_wo(2)
+        load_wo(3)
+        for i in range(3, T_TILES):
+            load_x(i)
+            load_o(i)
+
         gn_rows_f32 = keep.tile([P, P], F32)
         nc.vector.tensor_copy(out=gn_rows_f32[:], in_=gn_rows[:])
-        gn_t = psum_tr.tile([P, PACK, P], F32, tag="tr")
+        gn_t = psum_xt.tile([P, PACK, P], F32, tag="xt")
         nc.tensor.transpose(gn_t[:, 0, :], gn_rows_f32[:], ident[:])
         gn_cols = keep.tile([P, PACK], F32)
         nc.vector.tensor_copy(out=gn_cols[:], in_=gn_t[:, 0, 0:PACK])
@@ -91,20 +101,35 @@ def tile_multiscaleretention_pc_kernel(tc, o_ret, x, Wg, gn_weight, Wo, out):
         x_words = x_raw[:].bitcast(F32)
         x_codes = keep.tile([P, T_TILES, E_PASSES, P], U32, align_bytes=64)
         x_scales = keep.tile([P, T_TILES, E_PASSES, P], U8, align_bytes=64)
+        x_grouped = {}
+        rinv = {}
 
-        def prepare_x(i):
-            xt = psum_tr.tile([P, PACK, P], F32, tag="tr")
+        def transpose_x_and_norm(i):
+            xt = psum_xt.tile([P, PACK, P], F32, tag="xt")
             for cu in range(PACK):
                 nc.tensor.transpose(xt[:, cu, :], x_words[:, i, P * cu : P * (cu + 1)], ident[:])
-            x_grouped = pair.tile([P, E_PASSES, P, PACK], BF16, align_bytes=64)
-            nc.scalar.copy(
-                out=x_grouped[:].bitcast(F32),
-                in_=xt[:].rearrange("p (c u) t -> p c t u", u=2),
+            grouped = pair.tile([P, E_PASSES, P, PACK], BF16, align_bytes=64, tag="x_grouped")
+            nc.scalar.copy(out=grouped[:].bitcast(F32), in_=xt[:].rearrange("p (c u) t -> p c t u", u=2))
+            x_grouped[i] = grouped
+            ssq = keep.tile([P, HEADS], F32, name="ssq%d" % i)
+            for head in range(HEADS):
+                squares = pair.tile([P, DV], BF16, tag="squares")
+                nc.scalar.activation(
+                    out=squares[:],
+                    in_=o_raw[:, i, DV * head : DV * (head + 1)],
+                    func=ACT.Square,
+                    accum_out=ssq[:, head : head + 1],
+                )
+            rinv[i] = keep.tile([P, HEADS], F32, name="rinv%d" % i)
+            nc.scalar.activation(
+                out=rinv[i][:], in_=ssq[:], func=ACT.Abs_reciprocal_sqrt, scale=1.0 / DV, bias=eps_col[:]
             )
+
+        def quantise_x(i):
             nc.vector.quantize_mx(
                 out=x_codes[:, i, :, :].rearrange("p c t -> p (c t)").bitcast(FP8X4),
                 scales=x_scales[:, i, :, :].rearrange("p c t -> p (c t)"),
-                in_=x_grouped[:].rearrange("p c t j -> p (c t j)"),
+                in_=x_grouped[i][:].rearrange("p c t j -> p (c t j)"),
             )
 
         wg_codes = keep.tile([P, E_PASSES, F], U32, align_bytes=64)
@@ -112,86 +137,86 @@ def tile_multiscaleretention_pc_kernel(tc, o_ret, x, Wg, gn_weight, Wo, out):
         wo_codes = keep.tile([P, HEADS, N_OUT], U32, align_bytes=64)
         wo_scales = keep.tile([P, HEADS, N_OUT], U8, align_bytes=64)
 
-        for i in range(4):
-            prepare_x(i)
-        for c in range(E_PASSES):
-            for head in range(HEADS):
-                cols = slice(DV * head, DV * (head + 1))
-                copy = nc.vector.tensor_copy if head % 2 == 0 else nc.scalar.copy
-                regroup_and_quantise(
-                    nc, copy, stage, wg_raw[:, c, :, cols], wg_codes[:, c, cols], wg_scales[:, c, cols]
-                )
-        for i in range(4, T_TILES):
-            prepare_x(i)
+        def regroup(copy, rows):
+            grouped = w_stage.tile([P, N_TILE, PACK], BF16, align_bytes=64, tag="w_grouped")
+            copy(
+                out=grouped[:].rearrange("p (c i) j -> p c j i", i=4),
+                in_=rows.rearrange("p j (c i) -> p c j i", i=4),
+            )
+            return grouped
 
-        rinv = []
-        for i in range(T_TILES):
-            ssq = keep.tile([P, HEADS], F32, name="ssq%d" % i)
-            for head in range(HEADS):
-                squares = stage.tile([P, DV], BF16, tag="squares")
-                nc.scalar.activation(
-                    out=squares[:],
-                    in_=o_raw[:, i, DV * head : DV * (head + 1)],
-                    func=ACT.Square,
-                    accum_out=ssq[:, head : head + 1],
-                )
-            rms = keep.tile([P, HEADS], F32, name="rms%d" % i)
-            nc.scalar.activation(out=rms[:], in_=ssq[:], func=ACT.Sqrt, scale=1.0 / DV, bias=eps_col[:])
-            rinv_i = keep.tile([P, HEADS], F32, name="rinv%d" % i)
-            nc.vector.reciprocal(out=rinv_i[:], in_=rms[:])
-            rinv.append(rinv_i)
+        def quantise_weights(grouped, codes, scales):
+            nc.vector.quantize_mx(
+                out=codes.bitcast(FP8X4), scales=scales, in_=grouped[:].rearrange("p w j -> p (w j)")
+            )
 
-        for head in range(HEADS):
+        def prepare_wg(head_pair):
+            even, odd = 2 * head_pair, 2 * head_pair + 1
+            for c in range(E_PASSES):
+                on_vector = regroup(nc.vector.tensor_copy, wg_raw[:, c, :, DV * even : DV * (even + 1)])
+                on_scalar = regroup(nc.scalar.copy, wg_raw[:, c, :, DV * odd : DV * (odd + 1)])
+                for head, grouped in ((even, on_vector), (odd, on_scalar)):
+                    cols = slice(DV * head, DV * (head + 1))
+                    quantise_weights(grouped, wg_codes[:, c, cols], wg_scales[:, c, cols])
+
+        wo_grouped = {}
+
+        def regroup_wo_on_scalar(head):
+            wo_grouped[(head, 0)] = regroup(nc.scalar.copy, wo_raw[:, head, :, 0:N_TILE])
+
+        def regroup_wo_on_vector(head):
+            wo_grouped[(head, 1)] = regroup(nc.vector.tensor_copy, wo_raw[:, head, :, N_TILE:N_OUT])
+
+        def quantise_wo(head):
             for half in range(N_HALVES):
                 cols = slice(N_TILE * half, N_TILE * (half + 1))
-                regroup_and_quantise(
-                    nc,
-                    nc.scalar.copy,
-                    stage,
-                    wo_raw[:, head, :, cols],
-                    wo_codes[:, head, cols],
-                    wo_scales[:, head, cols],
-                )
+                quantise_weights(wo_grouped[(head, half)], wo_codes[:, head, cols], wo_scales[:, head, cols])
 
         h_codes = keep.tile([P, T_TILES, HEADS, P], U32, align_bytes=64)
         h_scales = keep.tile([P, T_TILES, HEADS, P], U8, align_bytes=64)
+        g_banks = {}
         h0_tiles = {}
+        ht_banks = {}
 
-        def gate_and_norm(i):
-            for head in range(HEADS):
-                cols = slice(DV * head, DV * (head + 1))
-                g = psum_g.tile([P, DV], F32)
-                for c in range(E_PASSES):
-                    nc.tensor.matmul_mx(
-                        out=g[:],
-                        lhsT=x_codes[:, i, c, :].bitcast(FP8X4),
-                        lhsT_scale=x_scales[:, i, c, :],
-                        rhs=wg_codes[:, c, cols].bitcast(FP8X4),
-                        rhs_scale=wg_scales[:, c, cols],
-                        start=(c == 0),
-                        stop=(c == E_PASSES - 1),
-                    )
-                h0 = h0_pool.tile([P, DV], F32)
-                nc.vector.scalar_tensor_tensor(
-                    out=h0[:],
-                    in0=g[:],
-                    scalar=rinv[i][:, head : head + 1],
-                    in1=o_raw[:, i, cols],
-                    op0=ALU.mult,
-                    op1=ALU.mult,
+        def gate_matmul(i, head):
+            cols = slice(DV * head, DV * (head + 1))
+            g = psum_g.tile([P, DV], F32, tag="g")
+            for c in range(E_PASSES):
+                nc.tensor.matmul_mx(
+                    out=g[:],
+                    lhsT=x_codes[:, i, c, :].bitcast(FP8X4),
+                    lhsT_scale=x_scales[:, i, c, :],
+                    rhs=wg_codes[:, c, cols].bitcast(FP8X4),
+                    rhs_scale=wg_scales[:, c, cols],
+                    start=(c == 0),
+                    stop=(c == E_PASSES - 1),
                 )
-                h0_tiles[(i, head)] = h0
+            g_banks[(i, head)] = g
 
-        def transpose_and_quantise(i):
-            h_grouped = pair.tile([P, HEADS, P, PACK], BF16, align_bytes=64)
+        def gate_times_norm(i, head):
+            h0 = h0_pool.tile([P, DV], F32, tag="h0")
+            nc.vector.scalar_tensor_tensor(
+                out=h0[:],
+                in0=g_banks[(i, head)][:],
+                scalar=rinv[i][:, head : head + 1],
+                in1=o_raw[:, i, DV * head : DV * (head + 1)],
+                op0=ALU.mult,
+                op1=ALU.mult,
+            )
+            h0_tiles[(i, head)] = h0
+
+        def transpose_h(i, head):
+            ht = psum_ht.tile([P, PACK, P], F32, tag="ht")
+            for j in range(PACK):
+                nc.tensor.transpose(ht[:, j, :], h0_tiles[(i, head)][:, P * j : P * (j + 1)], ident[:])
+            ht_banks[(i, head)] = ht
+
+        def weigh_and_quantise_h(i):
+            h_grouped = pair.tile([P, HEADS, P, PACK], BF16, align_bytes=64, tag="h_grouped")
             for head in range(HEADS):
-                h0 = h0_tiles[(i, head)]
-                ht = psum_tr.tile([P, PACK, P], F32, tag="tr")
-                for j in range(PACK):
-                    nc.tensor.transpose(ht[:, j, :], h0[:, P * j : P * (j + 1)], ident[:])
                 nc.vector.tensor_tensor(
                     out=h_grouped[:, head, :, :],
-                    in0=ht[:].rearrange("p j t -> p t j"),
+                    in0=ht_banks[(i, head)][:].rearrange("p j t -> p t j"),
                     in1=gn_cols[:].unsqueeze(1).to_broadcast([P, P, PACK]),
                     op=ALU.mult,
                 )
@@ -215,15 +240,42 @@ def tile_multiscaleretention_pc_kernel(tc, o_ret, x, Wg, gn_weight, Wo, out):
                         start=(head == 0),
                         stop=(head == HEADS - 1),
                     )
-            result = pair.tile([P, N_OUT], F32)
+            result = pair.tile([P, N_OUT], F32, tag="result")
             for half in range(N_HALVES):
                 nc.scalar.copy(out=result[:, N_TILE * half : N_TILE * (half + 1)], in_=acc[half][:])
             nc.sync.dma_start(out=out_view[:, i, :], in_=result[:])
 
+        transpose_x_and_norm(0)
+        quantise_x(0)
+        prepare_wg(0)
+        prepare_wg(1)
+
         for step in range(T_TILES + 2):
-            if step < T_TILES:
-                gate_and_norm(step)
+            if step + 1 < T_TILES:
+                transpose_x_and_norm(step + 1)
+            if step < 2:
+                regroup_wo_on_scalar(2 * step)
+                regroup_wo_on_scalar(2 * step + 1)
             if 1 <= step <= T_TILES:
-                transpose_and_quantise(step - 1)
+                for head in range(HEADS):
+                    transpose_h(step - 1, head)
+            if step < T_TILES:
+                gate_matmul(step, 0)
+                gate_matmul(step, 1)
             if step >= 2:
                 project_and_store(step - 2)
+            if step < T_TILES:
+                gate_matmul(step, 2)
+                gate_matmul(step, 3)
+            if 1 <= step <= T_TILES:
+                weigh_and_quantise_h(step - 1)
+            if step + 1 < T_TILES:
+                quantise_x(step + 1)
+            if step < T_TILES:
+                for head in range(HEADS):
+                    gate_times_norm(step, head)
+            if step < 2:
+                regroup_wo_on_vector(2 * step)
+                regroup_wo_on_vector(2 * step + 1)
+                quantise_wo(2 * step)
+                quantise_wo(2 * step + 1)

@@ -39,13 +39,15 @@ def tile_multiscaleretention_pc_kernel(tc, o_ret, x, Wg, gn_weight, Wo, out):
         name="psum_ht", bufs=3
     ) as psum_ht, tc.psum_pool(name="psum_xt", bufs=1) as psum_xt, tc.psum_pool(
         name="psum_acc", bufs=2
-    ) as psum_acc, tc.manual_schedule():
+    ) as psum_acc:
         ident = keep.tile([P, P], F32)
         make_identity(nc, ident[:])
         eps_col = keep.tile([P, 1], F32)
         nc.vector.memset(eps_col[:], EPS)
         gn_rows = keep.tile([P, P], BF16)
         nc.vector.memset(gn_rows[:], 0.0)
+        warm = keep.tile([P, 1], F32)
+        nc.scalar.activation(out=warm[:], in_=eps_col[:], func=ACT.Abs_reciprocal_sqrt)
 
         x_raw = keep.tile([P, T_TILES, E], BF16)
         wg_raw = keep.tile([P, E_PASSES, PACK, F], BF16)
@@ -109,7 +111,8 @@ def tile_multiscaleretention_pc_kernel(tc, o_ret, x, Wg, gn_weight, Wo, out):
             for cu in range(PACK):
                 nc.tensor.transpose(xt[:, cu, :], x_words[:, i, P * cu : P * (cu + 1)], ident[:])
             grouped = pair.tile([P, E_PASSES, P, PACK], BF16, align_bytes=64, tag="x_grouped")
-            nc.scalar.copy(out=grouped[:].bitcast(F32), in_=xt[:].rearrange("p (c u) t -> p c t u", u=2))
+            copy = nc.vector.tensor_copy if i < 2 else nc.scalar.copy
+            copy(out=grouped[:].bitcast(F32), in_=xt[:].rearrange("p (c u) t -> p c t u", u=2))
             x_grouped[i] = grouped
             ssq = keep.tile([P, HEADS], F32, name="ssq%d" % i)
             for head in range(HEADS):

import concourse.mybir as mybir
from concourse.masks import make_identity

FP8X4 = mybir.dt.float8_e4m3fn_x4
BF16 = mybir.dt.bfloat16
F32 = mybir.dt.float32
U32 = mybir.dt.uint32
U8 = mybir.dt.uint8
ACT = mybir.ActivationFunctionType
ALU = mybir.AluOpType

P = 128
PACK = 4
K_PASS = P * PACK
T = 1024
E = 1024
HEADS = 4
DV = 512
F = HEADS * DV
N_OUT = 1024
N_TILE = 512
T_TILES = T // P
E_PASSES = E // K_PASS
N_HALVES = N_OUT // N_TILE
EPS = 1e-5

FLOPS = 2 * T * E * F + 2 * T * F * N_OUT


def tile_multiscaleretention_pc_kernel(tc, o_ret, x, Wg, gn_weight, Wo, out):
    nc = tc.nc
    x_view = x.flatten_outer_dims().rearrange("(p i) e -> p i e", i=T_TILES)
    o_view = o_ret.rearrange("b t h d -> (b t) (h d)").rearrange("(p i) f -> p i f", i=T_TILES)
    out_view = out.flatten_outer_dims().rearrange("(p i) n -> p i n", i=T_TILES)

    with tc.tile_pool(name="keep", bufs=1) as keep, tc.tile_pool(name="w_stage", bufs=4) as w_stage, tc.tile_pool(
        name="h0_pool", bufs=2 * HEADS
    ) as h0_pool, tc.tile_pool(name="pair", bufs=2) as pair, tc.psum_pool(name="psum_g", bufs=2) as psum_g, tc.psum_pool(
        name="psum_ht", bufs=3
    ) as psum_ht, tc.psum_pool(name="psum_xt", bufs=1) as psum_xt, tc.psum_pool(
        name="psum_acc", bufs=2
    ) as psum_acc:
        ident = keep.tile([P, P], F32)
        make_identity(nc, ident[:])
        eps_col = keep.tile([P, 1], F32)
        nc.vector.memset(eps_col[:], EPS)
        gn_rows = keep.tile([P, P], BF16)
        nc.vector.memset(gn_rows[:], 0.0)
        warm = keep.tile([P, 1], F32)
        nc.scalar.activation(out=warm[:], in_=eps_col[:], func=ACT.Abs_reciprocal_sqrt)

        x_raw = keep.tile([P, T_TILES, E], BF16)
        wg_raw = keep.tile([P, E_PASSES, PACK, F], BF16)
        o_raw = keep.tile([P, T_TILES, F], BF16)
        wo_raw = keep.tile([P, HEADS, PACK, N_OUT], BF16)

        def load_x(i):
            nc.sync.dma_start(out=x_raw[:, i, :], in_=x_view[:, i, :])

        def load_o(i):
            nc.sync.dma_start(out=o_raw[:, i, :], in_=o_view[:, i, :])

        def load_wg(head_pair):
            cols = slice(2 * DV * head_pair, 2 * DV * (head_pair + 1))
            for c in range(E_PASSES):
                for u in range(2):
                    first = K_PASS * c + 256 * u
                    nc.sync.dma_start(
                        out=wg_raw[:, c, 2 * u : 2 * u + 2, cols],
                        in_=Wg[first : first + 256, cols].rearrange("(q e) f -> q e f", e=2),
                    )

        def load_wo(head):
            nc.sync.dma_start(
                out=wo_raw[:, head, :, :],
                in_=Wo[K_PASS * head : K_PASS * (head + 1), :].rearrange("(j p) n -> p j n", p=P),
            )

        nc.sync.dma_start(out=gn_rows[0:PACK, :], in_=gn_weight.rearrange("(j p) -> j p", p=P))
        load_x(0)
        load_o(0)
        load_x(1)
        load_wg(0)
        load_wg(1)
        load_o(1)
        load_wo(0)
        load_wo(1)
        load_x(2)
        load_o(2)
        load_wo(2)
        load_wo(3)
        for i in range(3, T_TILES):
            load_x(i)
            load_o(i)

        gn_rows_f32 = keep.tile([P, P], F32)
        nc.vector.tensor_copy(out=gn_rows_f32[:], in_=gn_rows[:])
        gn_t = psum_xt.tile([P, PACK, P], F32, tag="xt")
        nc.tensor.transpose(gn_t[:, 0, :], gn_rows_f32[:], ident[:])
        gn_cols = keep.tile([P, PACK], F32)
        nc.vector.tensor_copy(out=gn_cols[:], in_=gn_t[:, 0, 0:PACK])

        x_words = x_raw[:].bitcast(F32)
        x_codes = keep.tile([P, T_TILES, E_PASSES, P], U32, align_bytes=64)
        x_scales = keep.tile([P, T_TILES, E_PASSES, P], U8, align_bytes=64)
        x_grouped = {}
        rinv = {}

        def transpose_x_and_norm(i):
            xt = psum_xt.tile([P, PACK, P], F32, tag="xt")
            for cu in range(PACK):
                nc.tensor.transpose(xt[:, cu, :], x_words[:, i, P * cu : P * (cu + 1)], ident[:])
            grouped = pair.tile([P, E_PASSES, P, PACK], BF16, align_bytes=64, tag="x_grouped")
            copy = nc.vector.tensor_copy if i < 2 else nc.scalar.copy
            copy(out=grouped[:].bitcast(F32), in_=xt[:].rearrange("p (c u) t -> p c t u", u=2))
            x_grouped[i] = grouped
            ssq = keep.tile([P, HEADS], F32, name="ssq%d" % i)
            for head in range(HEADS):
                squares = pair.tile([P, DV], BF16, tag="squares")
                nc.scalar.activation(
                    out=squares[:],
                    in_=o_raw[:, i, DV * head : DV * (head + 1)],
                    func=ACT.Square,
                    accum_out=ssq[:, head : head + 1],
                )
            rinv[i] = keep.tile([P, HEADS], F32, name="rinv%d" % i)
            nc.scalar.activation(
                out=rinv[i][:], in_=ssq[:], func=ACT.Abs_reciprocal_sqrt, scale=1.0 / DV, bias=eps_col[:]
            )

        def quantise_x(i):
            nc.vector.quantize_mx(
                out=x_codes[:, i, :, :].rearrange("p c t -> p (c t)").bitcast(FP8X4),
                scales=x_scales[:, i, :, :].rearrange("p c t -> p (c t)"),
                in_=x_grouped[i][:].rearrange("p c t j -> p (c t j)"),
            )

        wg_codes = keep.tile([P, E_PASSES, F], U32, align_bytes=64)
        wg_scales = keep.tile([P, E_PASSES, F], U8, align_bytes=64)
        wo_codes = keep.tile([P, HEADS, N_OUT], U32, align_bytes=64)
        wo_scales = keep.tile([P, HEADS, N_OUT], U8, align_bytes=64)

        def regroup(copy, rows):
            grouped = w_stage.tile([P, N_TILE, PACK], BF16, align_bytes=64, tag="w_grouped")
            copy(
                out=grouped[:].rearrange("p (c i) j -> p c j i", i=4),
                in_=rows.rearrange("p j (c i) -> p c j i", i=4),
            )
            return grouped

        def quantise_weights(grouped, codes, scales):
            nc.vector.quantize_mx(
                out=codes.bitcast(FP8X4), scales=scales, in_=grouped[:].rearrange("p w j -> p (w j)")
            )

        def prepare_wg(head_pair):
            even, odd = 2 * head_pair, 2 * head_pair + 1
            for c in range(E_PASSES):
                on_vector = regroup(nc.vector.tensor_copy, wg_raw[:, c, :, DV * even : DV * (even + 1)])
                on_scalar = regroup(nc.scalar.copy, wg_raw[:, c, :, DV * odd : DV * (odd + 1)])
                for head, grouped in ((even, on_vector), (odd, on_scalar)):
                    cols = slice(DV * head, DV * (head + 1))
                    quantise_weights(grouped, wg_codes[:, c, cols], wg_scales[:, c, cols])

        wo_grouped = {}

        def regroup_wo_on_scalar(head):
            wo_grouped[(head, 0)] = regroup(nc.scalar.copy, wo_raw[:, head, :, 0:N_TILE])

        def regroup_wo_on_vector(head):
            wo_grouped[(head, 1)] = regroup(nc.vector.tensor_copy, wo_raw[:, head, :, N_TILE:N_OUT])

        def quantise_wo(head):
            for half in range(N_HALVES):
                cols = slice(N_TILE * half, N_TILE * (half + 1))
                quantise_weights(wo_grouped[(head, half)], wo_codes[:, head, cols], wo_scales[:, head, cols])

        h_codes = keep.tile([P, T_TILES, HEADS, P], U32, align_bytes=64)
        h_scales = keep.tile([P, T_TILES, HEADS, P], U8, align_bytes=64)
        g_banks = {}
        h0_tiles = {}
        ht_banks = {}

        def gate_matmul(i, head):
            cols = slice(DV * head, DV * (head + 1))
            g = psum_g.tile([P, DV], F32, tag="g")
            for c in range(E_PASSES):
                nc.tensor.matmul_mx(
                    out=g[:],
                    lhsT=x_codes[:, i, c, :].bitcast(FP8X4),
                    lhsT_scale=x_scales[:, i, c, :],
                    rhs=wg_codes[:, c, cols].bitcast(FP8X4),
                    rhs_scale=wg_scales[:, c, cols],
                    start=(c == 0),
                    stop=(c == E_PASSES - 1),
                )
            g_banks[(i, head)] = g

        def gate_times_norm(i, head):
            h0 = h0_pool.tile([P, DV], F32, tag="h0")
            nc.vector.scalar_tensor_tensor(
                out=h0[:],
                in0=g_banks[(i, head)][:],
                scalar=rinv[i][:, head : head + 1],
                in1=o_raw[:, i, DV * head : DV * (head + 1)],
                op0=ALU.mult,
                op1=ALU.mult,
            )
            h0_tiles[(i, head)] = h0

        def transpose_h(i, head):
            ht = psum_ht.tile([P, PACK, P], F32, tag="ht")
            for j in range(PACK):
                nc.tensor.transpose(ht[:, j, :], h0_tiles[(i, head)][:, P * j : P * (j + 1)], ident[:])
            ht_banks[(i, head)] = ht

        def weigh_and_quantise_h(i):
            h_grouped = pair.tile([P, HEADS, P, PACK], BF16, align_bytes=64, tag="h_grouped")
            for head in range(HEADS):
                nc.vector.tensor_tensor(
                    out=h_grouped[:, head, :, :],
                    in0=ht_banks[(i, head)][:].rearrange("p j t -> p t j"),
                    in1=gn_cols[:].unsqueeze(1).to_broadcast([P, P, PACK]),
                    op=ALU.mult,
                )
            nc.vector.quantize_mx(
                out=h_codes[:, i, :, :].rearrange("p h t -> p (h t)").bitcast(FP8X4),
                scales=h_scales[:, i, :, :].rearrange("p h t -> p (h t)"),
                in_=h_grouped[:].rearrange("p h t j -> p (h t j)"),
            )

        def project_and_store(i):
            acc = [psum_acc.tile([P, N_TILE], F32, name="acc%d" % half, tag="acc") for half in range(N_HALVES)]
            for head in range(HEADS):
                for half in range(N_HALVES):
                    cols = slice(N_TILE * half, N_TILE * (half + 1))
                    nc.tensor.matmul_mx(
                        out=acc[half][:],
                        lhsT=h_codes[:, i, head, :].bitcast(FP8X4),
                        lhsT_scale=h_scales[:, i, head, :],
                        rhs=wo_codes[:, head, cols].bitcast(FP8X4),
                        rhs_scale=wo_scales[:, head, cols],
                        start=(head == 0),
                        stop=(head == HEADS - 1),
                    )
            result = pair.tile([P, N_OUT], F32, tag="result")
            for half in range(N_HALVES):
                nc.scalar.copy(out=result[:, N_TILE * half : N_TILE * (half + 1)], in_=acc[half][:])
            nc.sync.dma_start(out=out_view[:, i, :], in_=result[:])

        transpose_x_and_norm(0)
        quantise_x(0)
        prepare_wg(0)
        prepare_wg(1)

        for step in range(T_TILES + 2):
            if step + 1 < T_TILES:
                transpose_x_and_norm(step + 1)
            if step < 2:
                regroup_wo_on_scalar(2 * step)
                regroup_wo_on_scalar(2 * step + 1)
            if 1 <= step <= T_TILES:
                for head in range(HEADS):
                    transpose_h(step - 1, head)
            if step < T_TILES:
                gate_matmul(step, 0)
                gate_matmul(step, 1)
            if step >= 2:
                project_and_store(step - 2)
            if step < T_TILES:
                gate_matmul(step, 2)
                gate_matmul(step, 3)
            if 1 <= step <= T_TILES:
                weigh_and_quantise_h(step - 1)
            if step + 1 < T_TILES:
                quantise_x(step + 1)
            if step < T_TILES:
                for head in range(HEADS):
                    gate_times_norm(step, head)
            if step < 2:
                regroup_wo_on_vector(2 * step)
                regroup_wo_on_vector(2 * step + 1)
                quantise_wo(2 * step)
                quantise_wo(2 * step + 1)
